import numpy as np
import ml_dtypes


def mxq(x, axis, fmt="e4m3"):
    dtype, down = {"e4m3": (ml_dtypes.float8_e4m3fn, 7), "e5m2": (ml_dtypes.float8_e5m2, 14)}[fmt]
    v = np.moveaxis(np.asarray(x, np.float32).astype(ml_dtypes.bfloat16).astype(np.float64), axis, -1)
    blocks = v.reshape(v.shape[:-1] + (-1, 32))
    amax = np.abs(blocks).max(-1, keepdims=True)
    byte = np.maximum(np.where(amax > 0, np.frexp(amax)[1] - 1 + 127, 0) - down, 1)
    scale = np.exp2(byte - 127.0)
    codes = (blocks / scale).astype(np.float32).astype(dtype).astype(np.float64)
    return np.moveaxis((codes * scale).reshape(v.shape), -1, axis)


WIDE = False


def mx_kscale(k):
    if not WIDE:
        return np.ones(k)
    levels = np.array([10, -10, 5, -5, 0])
    a = np.random.permutation(np.resize(levels, k // 512 * 4)).reshape(k // 512, 4)
    idx = np.arange(k)
    return np.exp2(a[idx // 512, idx % 128 // 32])


BF16 = ml_dtypes.bfloat16


def bf(x):
    return np.asarray(x, np.float32).astype(BF16)


def f64(x):
    return np.asarray(x).astype(np.float64)


E2M1 = np.array([0.0, 0.5, 1.0, 1.5, 2.0, 3.0, 4.0, 6.0, -0.0, -0.5, -1.0, -1.5, -2.0, -3.0, -4.0, -6.0])


def pack_weight(w, fmt):
    k, n = w.shape
    w = f64(bf(w)).reshape(k // 32, 32, n)
    amax = np.abs(w).max(1)
    if fmt == "e4m3":
        byte = np.frexp(amax)[1] - 1 + 127 - 7
    else:
        mant, ex = np.frexp(amax / 6.0)
        byte = np.where(mant > 0.5, ex, ex - 1) + 127
    byte = np.clip(np.where(amax > 0, byte, 1), 1, 254)
    scaled = (w * np.exp2(127.0 - byte)[:, None, :]).reshape(k, n).astype(np.float32)
    by_word = np.ascontiguousarray(scaled.reshape(k // 512, 128, 4, n).transpose(0, 1, 3, 2))
    if fmt == "e4m3":
        words = by_word.astype(ml_dtypes.float8_e4m3fn).view(np.uint8)
    else:
        c = by_word.astype(ml_dtypes.float4_e2m1fn).view(np.uint8) & 0xF
        words = c[..., 0::2] | (c[..., 1::2] << 4)
    return np.ascontiguousarray(words), np.ascontiguousarray(byte.astype(np.uint8).reshape(k // 512, 16, n))


def unpack_weight(words, scales, fmt):
    g, p, n, _ = words.shape
    if fmt == "e4m3":
        vals = np.ascontiguousarray(words).view(ml_dtypes.float8_e4m3fn).astype(np.float64)
    else:
        nib = np.empty((g, p, n, 4), np.uint8)
        nib[..., 0::2] = words & 0xF
        nib[..., 1::2] = words >> 4
        vals = E2M1[nib]
    vals = vals * np.repeat(np.exp2(scales.astype(np.float64) - 127.0), 8, axis=1)[..., None]
    return vals.transpose(0, 1, 3, 2).reshape(g * 512, n)

def pack4(w):
    words, scales = pack_weight(w, "e2m1")
    return words.reshape(words.shape[0], 128, -1), scales


def unpack4(words, scales):
    return unpack_weight(words.reshape(words.shape[0], 128, -1, 2), scales, "e2m1")


B, T, E, H, HKV, DH, WINDOW = 1, 1024, 2048, 8, 4, 128, 512
ROPE_THETA = 10000.0
EPS = 1e-6


def rms_norm(u, w):
    return u * (1.0 / np.sqrt(np.mean(u * u, axis=-1, keepdims=True) + EPS)) * (1.0 + w)


def rotate_half(u):
    return np.concatenate((-u[..., DH // 2:], u[..., :DH // 2]), axis=-1)


def setup_inputs():
    s = mx_kscale(E)
    x = bf(np.random.standard_normal((B, T, E)) * s)
    wq_words, wq_scales = pack4((np.random.standard_normal((H * DH, E)) / np.sqrt(E) / s).T)
    wk_words, wk_scales = pack4((np.random.standard_normal((HKV * DH, E)) / np.sqrt(E) / s).T)
    wv_words, wv_scales = pack4((np.random.standard_normal((HKV * DH, E)) * 2.0 / np.sqrt(E) / s).T)
    q_norm_w = bf(np.random.standard_normal(DH) * 0.1)
    k_norm_w = bf(np.random.standard_normal(DH) * 0.1)
    return {"x": x,
            "wq_words": wq_words, "wq_scales": wq_scales,
            "wk_words": wk_words, "wk_scales": wk_scales,
            "wv_words": wv_words, "wv_scales": wv_scales,
            "q_norm_w": q_norm_w,
            "k_norm_w": k_norm_w}


def reference(x, wq_words, wq_scales, wk_words, wk_scales, wv_words, wv_scales, q_norm_w, k_norm_w):
    xq = mxq(f64(x), 2, "e4m3")
    q = (xq @ unpack4(wq_words, wq_scales)).reshape(B, T, H, DH).transpose(0, 2, 1, 3)
    k = (xq @ unpack4(wk_words, wk_scales)).reshape(B, T, HKV, DH).transpose(0, 2, 1, 3)
    v = (xq @ unpack4(wv_words, wv_scales)).reshape(B, T, HKV, DH).transpose(0, 2, 1, 3)
    q = rms_norm(q, f64(q_norm_w))
    k = rms_norm(k, f64(k_norm_w))
    pos = f64(np.arange(T))
    inv_freq = 1.0 / (ROPE_THETA ** (f64(np.arange(0, DH, 2)) / DH))
    freqs = pos[:, None] * inv_freq[None, :]
    emb = np.concatenate((freqs, freqs), axis=-1)
    cos = np.cos(emb)[None, None, :, :]
    sin = np.sin(emb)[None, None, :, :]
    q = q * cos + rotate_half(q) * sin
    k = k * cos + rotate_half(k) * sin
    q = q * (DH ** -0.5)
    return q, k, v

@@ -1,0 +1,327 @@
+import math
+from contextlib import ExitStack
+
+import concourse.mybir as mybir
+from concourse.masks import make_identity
+
+F32 = mybir.dt.float32
+BF16 = mybir.dt.bfloat16
+I32 = mybir.dt.int32
+U32 = mybir.dt.uint32
+U8 = mybir.dt.uint8
+FP8X4 = mybir.dt.float8_e4m3fn_x4
+FP4X4 = mybir.dt.float4_e2m1fn_x4
+ALU = mybir.AluOpType
+ACT = mybir.ActivationFunctionType
+
+P = 128
+PACK = 4
+K_PASS = P * PACK
+T = 1024
+E = 2048
+DH = 128
+HALF = DH // 2
+DOUBLINGS = 6
+TILES = T // P
+PASSES = E // K_PASS
+CHUNK = 512
+CHUNK_HEADS = CHUNK // DH
+CHUNKS = 4
+ROPE_THETA = 10000.0
+EPS = 1e-6
+Q_SCALE = DH**-0.5
+TWO_PI = 2.0 * math.pi
+ROUND_MAGIC = 1.5 * 2.0**23
+
+FLOPS = 2 * T * E * (CHUNKS * CHUNK)
+
+assert 2**DOUBLINGS == HALF
+
+
+def tile_gemma3mhattention_pa_kernel(
+    tc,
+    x,
+    wq_words,
+    wq_scales,
+    wk_words,
+    wk_scales,
+    wv_words,
+    wv_scales,
+    q_norm_w,
+    k_norm_w,
+    out_0,
+    out_1,
+    out_2,
+):
+    nc = tc.nc
+
+    x_by_tile = x[0].rearrange("(p i) k -> i p k", i=TILES)
+    q_by_tile = out_0[0].rearrange("h (p i) d -> i p h d", i=TILES)
+    k_by_tile = out_1[0].rearrange("h (p i) d -> i p h d", i=TILES)
+    v_by_tile = out_2[0].rearrange("h (p i) d -> i p h d", i=TILES)
+    chunk_words = [
+        wq_words[:, :, 0 : 2 * CHUNK],
+        wq_words[:, :, 2 * CHUNK : 4 * CHUNK],
+        wk_words,
+        wv_words,
+    ]
+    chunk_scales = [
+        wq_scales[:, :, 0:CHUNK],
+        wq_scales[:, :, CHUNK : 2 * CHUNK],
+        wk_scales,
+        wv_scales,
+    ]
+    chunk_out = [
+        q_by_tile[:, :, 0:CHUNK_HEADS, :],
+        q_by_tile[:, :, CHUNK_HEADS : 2 * CHUNK_HEADS, :],
+        k_by_tile,
+        v_by_tile,
+    ]
+
+    with ExitStack() as stack:
+        stack.enter_context(tc.manual_schedule())
+        keep = stack.enter_context(tc.tile_pool(name="keep", bufs=1))
+        stage = stack.enter_context(tc.tile_pool(name="stage", bufs=3))
+        results = stack.enter_context(tc.tile_pool(name="results", bufs=6))
+        psum_xt = stack.enter_context(tc.psum_pool(name="psum_xt", bufs=2))
+        psum_acc = stack.enter_context(tc.psum_pool(name="psum_acc", bufs=6))
+
+        gain_rows = keep.tile([P, 2 * DH], BF16)
+        nc.vector.memset(gain_rows[:], 0.0)
+        nc.scalar.dma_start(out=gain_rows[0:1, 0:DH], in_=q_norm_w.rearrange("(o d) -> o d", o=1))
+        nc.scalar.dma_start(
+            out=gain_rows[0:1, DH : 2 * DH], in_=k_norm_w.rearrange("(o d) -> o d", o=1)
+        )
+        eps = keep.tile([P, 1], F32)
+        nc.vector.memset(eps[:], EPS)
+        warm = keep.tile([P, 1], F32)
+        nc.scalar.activation(out=warm[:], in_=eps[:], func=ACT.Sin)
+
+        x_tiles = [keep.tile([P, E], BF16, name="x%d" % i) for i in range(TILES)]
+        w_words = [
+            keep.tile([P, PASSES, 2 * CHUNK], U8, name="w_words%d" % c, align_bytes=64)
+            for c in range(CHUNKS)
+        ]
+        w_planes = [
+            keep.tile([P, PASSES, CHUNK], U8, name="w_planes%d" % c, align_bytes=64)
+            for c in range(CHUNKS)
+        ]
+
+        def load_x(i):
+            nc.sync.dma_start(out=x_tiles[i][:], in_=x_by_tile[i])
+
+        def load_words(c):
+            nc.sync.dma_start(
+                out=w_words[c][:].bitcast(I32),
+                in_=chunk_words[c].rearrange("g p b -> p g b").bitcast(I32),
+            )
+
+        def load_scales(c):
+            nc.vector.memset(w_planes[c][:].bitcast(I32), 0)
+            for quadrant in range(4):
+                nc.sync.dma_start(
+                    out=w_planes[c][32 * quadrant : 32 * quadrant + 4].bitcast(I32),
+                    in_=chunk_scales[c][:, 4 * quadrant : 4 * quadrant + 4, :]
+                    .rearrange("g r n -> r g n")
+                    .bitcast(I32),
+                )
+
+        load_x(0)
+        for c in range(CHUNKS):
+            load_scales(c)
+        load_words(0)
+        load_x(1)
+        for c in range(1, CHUNKS):
+            load_words(c)
+        for i in range(2, TILES):
+            load_x(i)
+
+        position_int = keep.tile([P, TILES], I32)
+        nc.gpsimd.iota(position_int[:], pattern=[[1, TILES]], base=0, channel_multiplier=TILES)
+        identity = keep.tile([P, P], F32)
+        make_identity(nc, identity[:])
+        ones = keep.tile([P, P], BF16)
+        nc.gpsimd.memset(ones[:], 1.0)
+
+        turns_per_step = keep.tile([P, HALF], F32)
+        nc.vector.memset(turns_per_step[:, 0:1], 1.0)
+        nc.vector.tensor_scalar(
+            out=turns_per_step[:, 0:1],
+            in0=turns_per_step[:, 0:1],
+            scalar1=1.0 / TWO_PI,
+            scalar2=None,
+            op0=ALU.mult,
+        )
+        for doubling in range(DOUBLINGS):
+            width = 2**doubling
+            nc.vector.tensor_scalar(
+                out=turns_per_step[:, width : 2 * width],
+                in0=turns_per_step[:, 0:width],
+                scalar1=ROPE_THETA ** (-width / HALF),
+                scalar2=None,
+                op0=ALU.mult,
+            )
+        position = keep.tile([P, TILES], F32)
+        nc.vector.tensor_copy(out=position[:], in_=position_int[:])
+
+        table_shape = [P, TILES, HALF]
+        turns = keep.tile(table_shape, F32)
+        nc.vector.tensor_tensor(
+            out=turns[:],
+            in0=position[:].unsqueeze(2).to_broadcast(table_shape),
+            in1=turns_per_step[:].unsqueeze(1).to_broadcast(table_shape),
+            op=ALU.mult,
+        )
+        whole_turns = keep.tile(table_shape, F32)
+        nc.vector.tensor_scalar(
+            out=whole_turns[:],
+            in0=turns[:],
+            scalar1=ROUND_MAGIC,
+            scalar2=ROUND_MAGIC,
+            op0=ALU.add,
+            op1=ALU.subtract,
+        )
+        part = keep.tile(table_shape, F32)
+        nc.vector.tensor_tensor(out=part[:], in0=turns[:], in1=whole_turns[:], op=ALU.subtract)
+        minus_abs = keep.tile(table_shape, F32)
+        nc.vector.scalar_tensor_tensor(
+            out=minus_abs[:], in0=part[:], scalar=-1.0, in1=part[:], op0=ALU.mult, op1=ALU.min
+        )
+        quarter_less = keep.tile(table_shape, F32)
+        nc.vector.tensor_scalar_add(out=quarter_less[:], in0=minus_abs[:], scalar1=0.25)
+
+        gain_psum = psum_acc.tile([P, CHUNK], F32, tag="acc")
+        nc.tensor.matmul(
+            out=gain_psum[:, 0 : 2 * DH], lhsT=ones[:], rhs=gain_rows[:], start=True, stop=True
+        )
+        gain_cos = keep.tile([P, 2, DH], F32)
+        gain_sin = keep.tile([P, 2, DH], F32)
+        for n, scale in ((0, Q_SCALE), (1, 1.0)):
+            low = slice(n * DH, n * DH + HALF)
+            high = slice(n * DH + HALF, (n + 1) * DH)
+            both = slice(n * DH, (n + 1) * DH)
+            nc.vector.tensor_scalar(
+                out=gain_cos[:, n, :], in0=gain_psum[:, both],
+                scalar1=1.0, scalar2=scale, op0=ALU.add, op1=ALU.mult,
+            )
+            nc.vector.tensor_scalar(
+                out=gain_sin[:, n, 0:HALF], in0=gain_psum[:, low],
+                scalar1=1.0, scalar2=scale, op0=ALU.add, op1=ALU.mult,
+            )
+            nc.vector.tensor_scalar(
+                out=gain_sin[:, n, HALF:DH], in0=gain_psum[:, high],
+                scalar1=1.0, scalar2=-scale, op0=ALU.add, op1=ALU.mult,
+            )
+
+        def transpose_and_quantise(i):
+            pairs = x_tiles[i][:].bitcast(F32)
+            x_words = stage.tile([P, PASSES, P], U32, align_bytes=64)
+            x_planes = stage.tile([P, PASSES, P], U8, align_bytes=64)
+            for first in range(0, PASSES, 2):
+                transposed = psum_xt.tile([P, 2, 2, P], F32)
+                for g in range(2):
+                    start = (first + g) * (K_PASS // 2)
+                    for u in range(2):
+                        nc.tensor.transpose(
+                            transposed[:, g, u, :],
+                            pairs[:, start + u : start + K_PASS // 2 : 2],
+                            identity[:],
+                        )
+                grouped = stage.tile([P, 2, P, PACK], BF16, align_bytes=64)
+                nc.scalar.copy(
+                    out=grouped[:].bitcast(F32), in_=transposed[:].rearrange("p g u m -> p g m u")
+                )
+                nc.vector.quantize_mx(
+                    out=x_words[:, first : first + 2, :].rearrange("p g m -> p (g m)").bitcast(FP8X4),
+                    scales=x_planes[:, first : first + 2, :].rearrange("p g m -> p (g m)"),
+                    in_=grouped[:].rearrange("p g m t -> p (g m t)"),
+                )
+            return x_words, x_planes
+
+        def project(x_words, x_planes, c):
+            acc = psum_acc.tile([P, CHUNK], F32)
+            for g in range(PASSES):
+                nc.tensor.matmul_mx(
+                    out=acc[:],
+                    lhsT=x_words[:, g, :].bitcast(FP8X4),
+                    lhsT_scale=x_planes[:, g, :],
+                    rhs=w_words[c][:, g, :].bitcast(FP4X4),
+                    rhs_scale=w_planes[c][:, g, :],
+                    start=(g == 0),
+                    stop=(g == PASSES - 1),
+                )
+            return acc
+
+        def norm_and_rope(i, c, acc, cos_table, sin_table):
+            squares = stage.tile([P, CHUNK], BF16)
+            sum_squares = stage.tile([P, CHUNK_HEADS], F32)
+            for h in range(CHUNK_HEADS):
+                head = slice(h * DH, (h + 1) * DH)
+                nc.scalar.activation(
+                    out=squares[:, head], in_=acc[:, head], func=ACT.Square,
+                    accum_out=sum_squares[:, h : h + 1],
+                )
+            rms = stage.tile([P, CHUNK_HEADS], F32)
+            nc.scalar.activation(
+                out=rms[:], in_=sum_squares[:], func=ACT.Sqrt, bias=eps[:], scale=1.0 / DH
+            )
+            rstd = stage.tile([P, CHUNK_HEADS], F32)
+            nc.vector.reciprocal(out=rstd[:], in_=rms[:])
+            straight = results.tile([P, CHUNK_HEADS, 2, HALF], F32)
+            crossed = stage.tile([P, CHUNK_HEADS, 2, HALF], F32)
+            for product, table in ((straight, cos_table), (crossed, sin_table)):
+                for h in range(CHUNK_HEADS):
+                    nc.vector.scalar_tensor_tensor(
+                        out=product[:, h].rearrange("p a j -> p (a j)"),
+                        in0=acc[:, h * DH : (h + 1) * DH],
+                        scalar=rstd[:, h : h + 1],
+                        in1=table[:, i, :],
+                        op0=ALU.mult,
+                        op1=ALU.mult,
+                    )
+            for a in range(2):
+                nc.gpsimd.tensor_tensor(
+                    out=straight[:, :, a, :], in0=straight[:, :, a, :], in1=crossed[:, :, 1 - a, :],
+                    op=ALU.add,
+                )
+            nc.sync.dma_start(out=chunk_out[c][i], in_=straight[:].rearrange("p h a j -> p h (a j)"))
+
+        def copy_out(i, c, acc):
+            plain = results.tile([P, CHUNK_HEADS, DH], F32)
+            nc.scalar.copy(out=plain[:].rearrange("p h d -> p (h d)"), in_=acc[:])
+            nc.sync.dma_start(out=chunk_out[c][i], in_=plain[:])
+
+        operand = transpose_and_quantise(0)
+
+        sin = keep.tile(table_shape, F32)
+        nc.scalar.activation(out=sin[:], in_=part[:], func=ACT.Sin, scale=TWO_PI)
+        cos = keep.tile(table_shape, F32)
+        nc.scalar.activation(out=cos[:], in_=quarter_less[:], func=ACT.Sin, scale=TWO_PI)
+        nc.scalar.activation(out=warm[:], in_=eps[:], func=ACT.Sqrt)
+
+        full_shape = [P, TILES, 2, HALF]
+        tables = []
+        for n, engine in ((0, nc.vector), (1, nc.gpsimd)):
+            pair = []
+            for trig, gain, name in ((cos, gain_cos, "cos_table%d" % n), (sin, gain_sin, "sin_table%d" % n)):
+                table = keep.tile([P, TILES, DH], F32, name=name)
+                engine.tensor_tensor(
+                    out=table[:].rearrange("p i (a j) -> p i a j", a=2),
+                    in0=trig[:].unsqueeze(2).to_broadcast(full_shape),
+                    in1=gain[:, n, :].rearrange("p (a j) -> p a j", a=2).unsqueeze(1).to_broadcast(full_shape),
+                    op=ALU.mult,
+                )
+                pair.append(table)
+            tables.append(pair)
+        chunk_tables = [tables[0], tables[0], tables[1]]
+
+        for i in range(TILES):
+            x_words, x_planes = operand
+            for c in range(CHUNKS):
+                acc = project(x_words, x_planes, c)
+                if c < CHUNKS - 1:
+                    norm_and_rope(i, c, acc, chunk_tables[c][0], chunk_tables[c][1])
+                else:
+                    copy_out(i, c, acc)
+                if c == 0 and i + 1 < TILES:
+                    operand = transpose_and_quantise(i + 1)

@@ -65,12 +65,7 @@ def tile_gemma3mhattention_pa_kernel(
         wk_words,
         wv_words,
     ]
-    chunk_scales = [
-        wq_scales[:, :, 0:CHUNK],
-        wq_scales[:, :, CHUNK : 2 * CHUNK],
-        wk_scales,
-        wv_scales,
-    ]
+    weight_scales = [wq_scales, wk_scales, wv_scales]
     chunk_out = [
         q_by_tile[:, :, 0:CHUNK_HEADS, :],
         q_by_tile[:, :, CHUNK_HEADS : 2 * CHUNK_HEADS, :],
@@ -86,29 +81,27 @@ def tile_gemma3mhattention_pa_kernel(
         psum_xt = stack.enter_context(tc.psum_pool(name="psum_xt", bufs=2))
         psum_acc = stack.enter_context(tc.psum_pool(name="psum_acc", bufs=6))
 
-        gain_rows = keep.tile([P, 2 * DH], BF16)
-        nc.vector.memset(gain_rows[:], 0.0)
-        nc.scalar.dma_start(out=gain_rows[0:1, 0:DH], in_=q_norm_w.rearrange("(o d) -> o d", o=1))
-        nc.scalar.dma_start(
-            out=gain_rows[0:1, DH : 2 * DH], in_=k_norm_w.rearrange("(o d) -> o d", o=1)
-        )
-        eps = keep.tile([P, 1], F32)
-        nc.vector.memset(eps[:], EPS)
-        warm = keep.tile([P, 1], F32)
-        nc.scalar.activation(out=warm[:], in_=eps[:], func=ACT.Sin)
-
         x_tiles = [keep.tile([P, E], BF16, name="x%d" % i) for i in range(TILES)]
         w_words = [
             keep.tile([P, PASSES, 2 * CHUNK], U8, name="w_words%d" % c, align_bytes=64)
             for c in range(CHUNKS)
         ]
+        plane_tiles = [
+            keep.tile([P, PASSES, width], U8, name="planes_%s" % name, align_bytes=64)
+            for name, width in (("q", 2 * CHUNK), ("k", CHUNK), ("v", CHUNK))
+        ]
         w_planes = [
-            keep.tile([P, PASSES, CHUNK], U8, name="w_planes%d" % c, align_bytes=64)
-            for c in range(CHUNKS)
+            plane_tiles[0][:, :, 0:CHUNK],
+            plane_tiles[0][:, :, CHUNK : 2 * CHUNK],
+            plane_tiles[1][:],
+            plane_tiles[2][:],
         ]
 
-        def load_x(i):
-            nc.sync.dma_start(out=x_tiles[i][:], in_=x_by_tile[i])
+        def load_x(i, pieces):
+            width = E // pieces
+            for piece in range(pieces):
+                columns = slice(piece * width, (piece + 1) * width)
+                nc.sync.dma_start(out=x_tiles[i][:, columns], in_=x_by_tile[i][:, columns])
 
         def load_words(c):
             nc.sync.dma_start(
@@ -116,32 +109,64 @@ def tile_gemma3mhattention_pa_kernel(
                 in_=chunk_words[c].rearrange("g p b -> p g b").bitcast(I32),
             )
 
-        def load_scales(c):
-            nc.vector.memset(w_planes[c][:].bitcast(I32), 0)
+        def load_scales(n):
+            nc.gpsimd.memset(plane_tiles[n][:].bitcast(F32), 0.0)
             for quadrant in range(4):
                 nc.sync.dma_start(
-                    out=w_planes[c][32 * quadrant : 32 * quadrant + 4].bitcast(I32),
-                    in_=chunk_scales[c][:, 4 * quadrant : 4 * quadrant + 4, :]
+                    out=plane_tiles[n][32 * quadrant : 32 * quadrant + 4].bitcast(I32),
+                    in_=weight_scales[n][:, 4 * quadrant : 4 * quadrant + 4, :]
                     .rearrange("g r n -> r g n")
                     .bitcast(I32),
                 )
 
-        load_x(0)
-        for c in range(CHUNKS):
-            load_scales(c)
+        gain_rows = [keep.tile([P, DH], BF16, name="gain_rows%d" % n) for n in range(2)]
+        gain = [keep.tile([P, DH], F32, name="gain%d" % n) for n in range(2)]
+        for n in range(2):
+            nc.vector.memset(gain_rows[n][:], 0.0)
+
+        def load_gain(n):
+            nc.sync.dma_start(
+                out=gain_rows[n][0:1, :], in_=(q_norm_w, k_norm_w)[n].rearrange("(o d) -> o d", o=1)
+            )
+
+        def spread_gain(n):
+            scale = (Q_SCALE, 1.0)[n]
+            gain_psum = psum_acc.tile([P, CHUNK], F32, tag="acc")
+            nc.tensor.matmul(
+                out=gain_psum[:, 0:DH], lhsT=ones[:], rhs=gain_rows[n][:], start=True, stop=True
+            )
+            nc.scalar.activation(
+                out=gain[n][:], in_=gain_psum[:, 0:DH], func=ACT.Identity, scale=scale, bias=scale
+            )
+
+        eps = keep.tile([P, 1], F32)
+        nc.vector.memset(eps[:], EPS)
+        warm = keep.tile([P, 1], F32)
+        nc.scalar.activation(out=warm[:], in_=eps[:], func=ACT.Sin)
+
+        load_x(0, 2)
+        load_gain(0)
+        load_scales(0)
         load_words(0)
-        load_x(1)
-        for c in range(1, CHUNKS):
-            load_words(c)
-        for i in range(2, TILES):
-            load_x(i)
+        load_x(1, 1)
+        load_gain(1)
+        load_words(1)
 
         position_int = keep.tile([P, TILES], I32)
         nc.gpsimd.iota(position_int[:], pattern=[[1, TILES]], base=0, channel_multiplier=TILES)
-        identity = keep.tile([P, P], F32)
-        make_identity(nc, identity[:])
         ones = keep.tile([P, P], BF16)
         nc.gpsimd.memset(ones[:], 1.0)
+        identity = keep.tile([P, P], F32)
+        make_identity(nc, identity[:])
+
+        load_scales(1)
+        load_scales(2)
+        load_words(2)
+        load_words(3)
+        for i in range(2, TILES):
+            load_x(i, 1)
+
+        spread_gain(0)
 
         turns_per_step = keep.tile([P, HALF], F32)
         nc.vector.memset(turns_per_step[:, 0:1], 1.0)
@@ -183,40 +208,21 @@ def tile_gemma3mhattention_pa_kernel(
         )
         part = keep.tile(table_shape, F32)
         nc.vector.tensor_tensor(out=part[:], in0=turns[:], in1=whole_turns[:], op=ALU.subtract)
-        minus_abs = keep.tile(table_shape, F32)
-        nc.vector.scalar_tensor_tensor(
-            out=minus_abs[:], in0=part[:], scalar=-1.0, in1=part[:], op0=ALU.mult, op1=ALU.min
+        sin = keep.tile(table_shape, F32)
+        nc.scalar.activation(out=sin[:], in_=part[:], func=ACT.Sin, scale=TWO_PI)
+        abs_part = keep.tile(table_shape, F32)
+        nc.scalar.activation(out=abs_part[:], in_=part[:], func=ACT.Abs)
+        cos = keep.tile(table_shape, F32)
+        nc.scalar.activation(
+            out=cos[:], in_=abs_part[:], func=ACT.Sin, scale=-TWO_PI, bias=math.pi / 2.0
         )
-        quarter_less = keep.tile(table_shape, F32)
-        nc.vector.tensor_scalar_add(out=quarter_less[:], in0=minus_abs[:], scalar1=0.25)
-
-        gain_psum = psum_acc.tile([P, CHUNK], F32, tag="acc")
-        nc.tensor.matmul(
-            out=gain_psum[:, 0 : 2 * DH], lhsT=ones[:], rhs=gain_rows[:], start=True, stop=True
-        )
-        gain_cos = keep.tile([P, 2, DH], F32)
-        gain_sin = keep.tile([P, 2, DH], F32)
-        for n, scale in ((0, Q_SCALE), (1, 1.0)):
-            low = slice(n * DH, n * DH + HALF)
-            high = slice(n * DH + HALF, (n + 1) * DH)
-            both = slice(n * DH, (n + 1) * DH)
-            nc.vector.tensor_scalar(
-                out=gain_cos[:, n, :], in0=gain_psum[:, both],
-                scalar1=1.0, scalar2=scale, op0=ALU.add, op1=ALU.mult,
-            )
-            nc.vector.tensor_scalar(
-                out=gain_sin[:, n, 0:HALF], in0=gain_psum[:, low],
-                scalar1=1.0, scalar2=scale, op0=ALU.add, op1=ALU.mult,
-            )
-            nc.vector.tensor_scalar(
-                out=gain_sin[:, n, HALF:DH], in0=gain_psum[:, high],
-                scalar1=1.0, scalar2=-scale, op0=ALU.add, op1=ALU.mult,
-            )
+        nc.scalar.activation(out=warm[:], in_=eps[:], func=ACT.Abs_reciprocal_sqrt)
 
         def transpose_and_quantise(i):
             pairs = x_tiles[i][:].bitcast(F32)
             x_words = stage.tile([P, PASSES, P], U32, align_bytes=64)
             x_planes = stage.tile([P, PASSES, P], U8, align_bytes=64)
+            halves = []
             for first in range(0, PASSES, 2):
                 transposed = psum_xt.tile([P, 2, 2, P], F32)
                 for g in range(2):
@@ -228,9 +234,16 @@ def tile_gemma3mhattention_pa_kernel(
                             identity[:],
                         )
                 grouped = stage.tile([P, 2, P, PACK], BF16, align_bytes=64)
-                nc.scalar.copy(
-                    out=grouped[:].bitcast(F32), in_=transposed[:].rearrange("p g u m -> p g m u")
-                )
+                if i == 0:
+                    nc.vector.tensor_copy(
+                        out=grouped[:].bitcast(F32), in_=transposed[:].rearrange("p g u m -> p g m u")
+                    )
+                else:
+                    nc.scalar.copy(
+                        out=grouped[:].bitcast(F32), in_=transposed[:].rearrange("p g u m -> p g m u")
+                    )
+                halves.append((first, grouped))
+            for first, grouped in halves:
                 nc.vector.quantize_mx(
                     out=x_words[:, first : first + 2, :].rearrange("p g m -> p (g m)").bitcast(FP8X4),
                     scales=x_planes[:, first : first + 2, :].rearrange("p g m -> p (g m)"),
@@ -261,12 +274,11 @@ def tile_gemma3mhattention_pa_kernel(
                     out=squares[:, head], in_=acc[:, head], func=ACT.Square,
                     accum_out=sum_squares[:, h : h + 1],
                 )
-            rms = stage.tile([P, CHUNK_HEADS], F32)
-            nc.scalar.activation(
-                out=rms[:], in_=sum_squares[:], func=ACT.Sqrt, bias=eps[:], scale=1.0 / DH
-            )
             rstd = stage.tile([P, CHUNK_HEADS], F32)
-            nc.vector.reciprocal(out=rstd[:], in_=rms[:])
+            nc.scalar.activation(
+                out=rstd[:], in_=sum_squares[:], func=ACT.Abs_reciprocal_sqrt, bias=eps[:],
+                scale=1.0 / DH,
+            )
             straight = results.tile([P, CHUNK_HEADS, 2, HALF], F32)
             crossed = stage.tile([P, CHUNK_HEADS, 2, HALF], F32)
             for product, table in ((straight, cos_table), (crossed, sin_table)):
@@ -279,10 +291,10 @@ def tile_gemma3mhattention_pa_kernel(
                         op0=ALU.mult,
                         op1=ALU.mult,
                     )
-            for a in range(2):
+            for a, op in ((0, ALU.subtract), (1, ALU.add)):
                 nc.gpsimd.tensor_tensor(
                     out=straight[:, :, a, :], in0=straight[:, :, a, :], in1=crossed[:, :, 1 - a, :],
-                    op=ALU.add,
+                    op=op,
                 )
             nc.sync.dma_start(out=chunk_out[c][i], in_=straight[:].rearrange("p h a j -> p h (a j)"))
 
@@ -291,36 +303,34 @@ def tile_gemma3mhattention_pa_kernel(
             nc.scalar.copy(out=plain[:].rearrange("p h d -> p (h d)"), in_=acc[:])
             nc.sync.dma_start(out=chunk_out[c][i], in_=plain[:])
 
-        operand = transpose_and_quantise(0)
-
-        sin = keep.tile(table_shape, F32)
-        nc.scalar.activation(out=sin[:], in_=part[:], func=ACT.Sin, scale=TWO_PI)
-        cos = keep.tile(table_shape, F32)
-        nc.scalar.activation(out=cos[:], in_=quarter_less[:], func=ACT.Sin, scale=TWO_PI)
-        nc.scalar.activation(out=warm[:], in_=eps[:], func=ACT.Sqrt)
-
         full_shape = [P, TILES, 2, HALF]
-        tables = []
-        for n, engine in ((0, nc.vector), (1, nc.gpsimd)):
+
+        def build_tables(n, engine):
             pair = []
-            for trig, gain, name in ((cos, gain_cos, "cos_table%d" % n), (sin, gain_sin, "sin_table%d" % n)):
+            for trig, name in ((sin, "sin_table%d" % n), (cos, "cos_table%d" % n)):
                 table = keep.tile([P, TILES, DH], F32, name=name)
                 engine.tensor_tensor(
                     out=table[:].rearrange("p i (a j) -> p i a j", a=2),
                     in0=trig[:].unsqueeze(2).to_broadcast(full_shape),
-                    in1=gain[:, n, :].rearrange("p (a j) -> p a j", a=2).unsqueeze(1).to_broadcast(full_shape),
+                    in1=gain[n][:].rearrange("p (a j) -> p a j", a=2).unsqueeze(1).to_broadcast(full_shape),
                     op=ALU.mult,
                 )
                 pair.append(table)
-            tables.append(pair)
-        chunk_tables = [tables[0], tables[0], tables[1]]
+            return pair
+
+        operand = transpose_and_quantise(0)
+        q_tables = build_tables(0, nc.vector)
+        chunk_tables = [q_tables, q_tables]
 
         for i in range(TILES):
             x_words, x_planes = operand
             for c in range(CHUNKS):
                 acc = project(x_words, x_planes, c)
+                if i == 0 and c == 0:
+                    spread_gain(1)
+                    chunk_tables.append(build_tables(1, nc.gpsimd))
                 if c < CHUNKS - 1:
-                    norm_and_rope(i, c, acc, chunk_tables[c][0], chunk_tables[c][1])
+                    norm_and_rope(i, c, acc, chunk_tables[c][1], chunk_tables[c][0])
                 else:
                     copy_out(i, c, acc)
                 if c == 0 and i + 1 < TILES:

@@ -27,6 +27,7 @@ PASSES = E // K_PASS
 CHUNK = 512
 CHUNK_HEADS = CHUNK // DH
 CHUNKS = 4
+K_TABLES_SPLIT = 2
 ROPE_THETA = 10000.0
 EPS = 1e-6
 Q_SCALE = DH**-0.5
@@ -110,7 +111,10 @@ def tile_gemma3mhattention_pa_kernel(
             )
 
         def load_scales(n):
-            nc.gpsimd.memset(plane_tiles[n][:].bitcast(F32), 0.0)
+            if n == 0:
+                nc.vector.memset(plane_tiles[n][:].bitcast(I32), 0)
+            else:
+                nc.gpsimd.memset(plane_tiles[n][:].bitcast(F32), 0.0)
             for quadrant in range(4):
                 nc.sync.dma_start(
                     out=plane_tiles[n][32 * quadrant : 32 * quadrant + 4].bitcast(I32),
@@ -152,12 +156,24 @@ def tile_gemma3mhattention_pa_kernel(
         load_gain(1)
         load_words(1)
 
-        position_int = keep.tile([P, TILES], I32)
-        nc.gpsimd.iota(position_int[:], pattern=[[1, TILES]], base=0, channel_multiplier=TILES)
-        ones = keep.tile([P, P], BF16)
-        nc.gpsimd.memset(ones[:], 1.0)
         identity = keep.tile([P, P], F32)
         make_identity(nc, identity[:])
+        up_to = keep.tile([P, P], BF16)
+        nc.gpsimd.memset(up_to[:], 1.0)
+        nc.gpsimd.affine_select(
+            out=up_to[:], in_=up_to[:], compare_op=ALU.is_ge, fill=0.0, base=0, pattern=[[1, P]],
+            channel_multiplier=-1,
+        )
+        steps = keep.tile([P, TILES], BF16)
+        nc.gpsimd.memset(steps[:], float(TILES))
+        for i in range(TILES):
+            nc.gpsimd.memset(steps[0:1, i : i + 1], float(i))
+        ones = keep.tile([P, P], BF16)
+        nc.gpsimd.memset(ones[:], 1.0)
+        position_psum = psum_acc.tile([P, CHUNK], F32, tag="acc")
+        nc.tensor.matmul(
+            out=position_psum[:, 0:TILES], lhsT=up_to[:], rhs=steps[:], start=True, stop=True
+        )
 
         load_scales(1)
         load_scales(2)
@@ -187,7 +203,7 @@ def tile_gemma3mhattention_pa_kernel(
                 op0=ALU.mult,
             )
         position = keep.tile([P, TILES], F32)
-        nc.vector.tensor_copy(out=position[:], in_=position_int[:])
+        nc.vector.tensor_copy(out=position[:], in_=position_psum[:, 0:TILES])
 
         table_shape = [P, TILES, HALF]
         turns = keep.tile(table_shape, F32)
@@ -303,24 +319,24 @@ def tile_gemma3mhattention_pa_kernel(
             nc.scalar.copy(out=plain[:].rearrange("p h d -> p (h d)"), in_=acc[:])
             nc.sync.dma_start(out=chunk_out[c][i], in_=plain[:])
 
-        full_shape = [P, TILES, 2, HALF]
+        tables = [
+            [keep.tile([P, TILES, DH], F32, name="%s_table%d" % (name, n)) for name in ("sin", "cos")]
+            for n in range(2)
+        ]
 
-        def build_tables(n, engine):
-            pair = []
-            for trig, name in ((sin, "sin_table%d" % n), (cos, "cos_table%d" % n)):
-                table = keep.tile([P, TILES, DH], F32, name=name)
+        def fill_tables(n, engine, first, last):
+            shape = [P, last - first, 2, HALF]
+            for trig, table in zip((sin, cos), tables[n]):
                 engine.tensor_tensor(
-                    out=table[:].rearrange("p i (a j) -> p i a j", a=2),
-                    in0=trig[:].unsqueeze(2).to_broadcast(full_shape),
-                    in1=gain[n][:].rearrange("p (a j) -> p a j", a=2).unsqueeze(1).to_broadcast(full_shape),
+                    out=table[:, first:last, :].rearrange("p i (a j) -> p i a j", a=2),
+                    in0=trig[:, first:last, :].unsqueeze(2).to_broadcast(shape),
+                    in1=gain[n][:].rearrange("p (a j) -> p a j", a=2).unsqueeze(1).to_broadcast(shape),
                     op=ALU.mult,
                 )
-                pair.append(table)
-            return pair
 
         operand = transpose_and_quantise(0)
-        q_tables = build_tables(0, nc.vector)
-        chunk_tables = [q_tables, q_tables]
+        fill_tables(0, nc.vector, 0, TILES)
+        chunk_tables = [tables[0], tables[0], tables[1]]
 
         for i in range(TILES):
             x_words, x_planes = operand
@@ -328,7 +344,9 @@ def tile_gemma3mhattention_pa_kernel(
                 acc = project(x_words, x_planes, c)
                 if i == 0 and c == 0:
                     spread_gain(1)
-                    chunk_tables.append(build_tables(1, nc.gpsimd))
+                    fill_tables(1, nc.gpsimd, K_TABLES_SPLIT, TILES)
+                if i == 0 and c == 2:
+                    fill_tables(1, nc.vector, 0, K_TABLES_SPLIT)
                 if c < CHUNKS - 1:
                     norm_and_rope(i, c, acc, chunk_tables[c][1], chunk_tables[c][0])
                 else:

@@ -21,7 +21,8 @@ T = 1024
 E = 2048
 DH = 128
 HALF = DH // 2
-DOUBLINGS = 6
+SPREAD = 4
+POSITION_EXCESS = 9.0
 TILES = T // P
 PASSES = E // K_PASS
 CHUNK = 512
@@ -36,7 +37,7 @@ ROUND_MAGIC = 1.5 * 2.0**23
 
 FLOPS = 2 * T * E * (CHUNKS * CHUNK)
 
-assert 2**DOUBLINGS == HALF
+assert SPREAD**3 == HALF
 
 
 def tile_gemma3mhattention_pa_kernel(
@@ -125,8 +126,6 @@ def tile_gemma3mhattention_pa_kernel(
 
         gain_rows = [keep.tile([P, DH], BF16, name="gain_rows%d" % n) for n in range(2)]
         gain = [keep.tile([P, DH], F32, name="gain%d" % n) for n in range(2)]
-        for n in range(2):
-            nc.vector.memset(gain_rows[n][:], 0.0)
 
         def load_gain(n):
             nc.sync.dma_start(
@@ -147,34 +146,37 @@ def tile_gemma3mhattention_pa_kernel(
         nc.vector.memset(eps[:], EPS)
         warm = keep.tile([P, 1], F32)
         nc.scalar.activation(out=warm[:], in_=eps[:], func=ACT.Sin)
+        nc.vector.memset(gain_rows[0][:], 0.0)
 
         load_x(0, 2)
         load_gain(0)
         load_scales(0)
         load_words(0)
         load_x(1, 1)
-        load_gain(1)
-        load_words(1)
 
-        identity = keep.tile([P, P], F32)
-        make_identity(nc, identity[:])
         up_to = keep.tile([P, P], BF16)
         nc.gpsimd.memset(up_to[:], 1.0)
         nc.gpsimd.affine_select(
             out=up_to[:], in_=up_to[:], compare_op=ALU.is_ge, fill=0.0, base=0, pattern=[[1, P]],
             channel_multiplier=-1,
         )
-        steps = keep.tile([P, TILES], BF16)
-        nc.gpsimd.memset(steps[:], float(TILES))
-        for i in range(TILES):
-            nc.gpsimd.memset(steps[0:1, i : i + 1], float(i))
+        identity = keep.tile([P, P], F32)
+        make_identity(nc, identity[:])
         ones = keep.tile([P, P], BF16)
-        nc.gpsimd.memset(ones[:], 1.0)
+        nc.vector.memset(ones[:], 1.0)
+        eights = keep.tile([P, TILES], BF16)
+        nc.vector.memset(eights[:], float(TILES))
+        nc.vector.memset(gain_rows[1][:], 0.0)
         position_psum = psum_acc.tile([P, CHUNK], F32, tag="acc")
         nc.tensor.matmul(
-            out=position_psum[:, 0:TILES], lhsT=up_to[:], rhs=steps[:], start=True, stop=True
+            out=position_psum[:, 0:TILES], lhsT=up_to[:], rhs=eights[:], start=True, stop=False
+        )
+        nc.tensor.matmul(
+            out=position_psum[:, 0:TILES], lhsT=ones[:], rhs=up_to[:, 0:TILES], start=False, stop=True
         )
 
+        load_gain(1)
+        load_words(1)
         load_scales(1)
         load_scales(2)
         load_words(2)
@@ -182,28 +184,68 @@ def tile_gemma3mhattention_pa_kernel(
         for i in range(2, TILES):
             load_x(i, 1)
 
+        def transpose(i):
+            pairs = x_tiles[i][:].bitcast(F32)
+            halves = []
+            for first in range(0, PASSES, 2):
+                transposed = psum_xt.tile([P, 2, 2, P], F32)
+                for g in range(2):
+                    start = (first + g) * (K_PASS // 2)
+                    for u in range(2):
+                        nc.tensor.transpose(
+                            transposed[:, g, u, :],
+                            pairs[:, start + u : start + K_PASS // 2 : 2],
+                            identity[:],
+                        )
+                grouped = stage.tile([P, 2, P, PACK], BF16, align_bytes=64)
+                nc.scalar.copy(
+                    out=grouped[:].bitcast(F32), in_=transposed[:].rearrange("p g u m -> p g m u")
+                )
+                halves.append((first, grouped))
+            return halves
+
+        def quantise(halves):
+            x_words = stage.tile([P, PASSES, P], U32, align_bytes=64)
+            x_planes = stage.tile([P, PASSES, P], U8, align_bytes=64)
+            for first, grouped in halves:
+                nc.vector.quantize_mx(
+                    out=x_words[:, first : first + 2, :].rearrange("p g m -> p (g m)").bitcast(FP8X4),
+                    scales=x_planes[:, first : first + 2, :].rearrange("p g m -> p (g m)"),
+                    in_=grouped[:].rearrange("p g m t -> p (g m t)"),
+                )
+            return x_words, x_planes
+
         spread_gain(0)
+        first_halves = transpose(0)
 
         turns_per_step = keep.tile([P, HALF], F32)
-        nc.vector.memset(turns_per_step[:, 0:1], 1.0)
-        nc.vector.tensor_scalar(
-            out=turns_per_step[:, 0:1],
-            in0=turns_per_step[:, 0:1],
-            scalar1=1.0 / TWO_PI,
-            scalar2=None,
-            op0=ALU.mult,
-        )
-        for doubling in range(DOUBLINGS):
-            width = 2**doubling
+        one = keep.tile([P, 1], F32)
+        nc.vector.memset(one[:], 1.0)
+        for j in range(SPREAD):
             nc.vector.tensor_scalar(
-                out=turns_per_step[:, width : 2 * width],
-                in0=turns_per_step[:, 0:width],
-                scalar1=ROPE_THETA ** (-width / HALF),
+                out=turns_per_step[:, j : j + 1],
+                in0=one[:],
+                scalar1=ROPE_THETA ** (-j / HALF) / TWO_PI,
                 scalar2=None,
                 op0=ALU.mult,
             )
+        for width in (SPREAD, SPREAD * SPREAD):
+            for copy in range(1, SPREAD):
+                nc.vector.tensor_scalar(
+                    out=turns_per_step[:, copy * width : (copy + 1) * width],
+                    in0=turns_per_step[:, 0:width],
+                    scalar1=ROPE_THETA ** (-copy * width / HALF),
+                    scalar2=None,
+                    op0=ALU.mult,
+                )
         position = keep.tile([P, TILES], F32)
-        nc.vector.tensor_copy(out=position[:], in_=position_psum[:, 0:TILES])
+        nc.vector.tensor_scalar(
+            out=position[:],
+            in0=position_psum[:, 0:TILES],
+            scalar1=-POSITION_EXCESS,
+            scalar2=None,
+            op0=ALU.add,
+        )
 
         table_shape = [P, TILES, HALF]
         turns = keep.tile(table_shape, F32)
@@ -224,48 +266,15 @@ def tile_gemma3mhattention_pa_kernel(
         )
         part = keep.tile(table_shape, F32)
         nc.vector.tensor_tensor(out=part[:], in0=turns[:], in1=whole_turns[:], op=ALU.subtract)
-        sin = keep.tile(table_shape, F32)
-        nc.scalar.activation(out=sin[:], in_=part[:], func=ACT.Sin, scale=TWO_PI)
         abs_part = keep.tile(table_shape, F32)
         nc.scalar.activation(out=abs_part[:], in_=part[:], func=ACT.Abs)
+        sin = keep.tile(table_shape, F32)
+        nc.scalar.activation(out=sin[:], in_=part[:], func=ACT.Sin, scale=TWO_PI)
         cos = keep.tile(table_shape, F32)
         nc.scalar.activation(
             out=cos[:], in_=abs_part[:], func=ACT.Sin, scale=-TWO_PI, bias=math.pi / 2.0
         )
         nc.scalar.activation(out=warm[:], in_=eps[:], func=ACT.Abs_reciprocal_sqrt)
-
-        def transpose_and_quantise(i):
-            pairs = x_tiles[i][:].bitcast(F32)
-            x_words = stage.tile([P, PASSES, P], U32, align_bytes=64)
-            x_planes = stage.tile([P, PASSES, P], U8, align_bytes=64)
-            halves = []
-            for first in range(0, PASSES, 2):
-                transposed = psum_xt.tile([P, 2, 2, P], F32)
-                for g in range(2):
-                    start = (first + g) * (K_PASS // 2)
-                    for u in range(2):
-                        nc.tensor.transpose(
-                            transposed[:, g, u, :],
-                            pairs[:, start + u : start + K_PASS // 2 : 2],
-                            identity[:],
-                        )
-                grouped = stage.tile([P, 2, P, PACK], BF16, align_bytes=64)
-                if i == 0:
-                    nc.vector.tensor_copy(
-                        out=grouped[:].bitcast(F32), in_=transposed[:].rearrange("p g u m -> p g m u")
-                    )
-                else:
-                    nc.scalar.copy(
-                        out=grouped[:].bitcast(F32), in_=transposed[:].rearrange("p g u m -> p g m u")
-                    )
-                halves.append((first, grouped))
-            for first, grouped in halves:
-                nc.vector.quantize_mx(
-                    out=x_words[:, first : first + 2, :].rearrange("p g m -> p (g m)").bitcast(FP8X4),
-                    scales=x_planes[:, first : first + 2, :].rearrange("p g m -> p (g m)"),
-                    in_=grouped[:].rearrange("p g m t -> p (g m t)"),
-                )
-            return x_words, x_planes
 
         def project(x_words, x_planes, c):
             acc = psum_acc.tile([P, CHUNK], F32)
@@ -334,7 +343,7 @@ def tile_gemma3mhattention_pa_kernel(
                     op=ALU.mult,
                 )
 
-        operand = transpose_and_quantise(0)
+        operand = quantise(first_halves)
         fill_tables(0, nc.vector, 0, TILES)
         chunk_tables = [tables[0], tables[0], tables[1]]
 
@@ -352,4 +361,4 @@ def tile_gemma3mhattention_pa_kernel(
                 else:
                     copy_out(i, c, acc)
                 if c == 0 and i + 1 < TILES:
-                    operand = transpose_and_quantise(i + 1)
+                    operand = quantise(transpose(i + 1))

@@ -125,7 +125,8 @@ def tile_gemma3mhattention_pa_kernel(
                 )
 
         gain_rows = [keep.tile([P, DH], BF16, name="gain_rows%d" % n) for n in range(2)]
-        gain = [keep.tile([P, DH], F32, name="gain%d" % n) for n in range(2)]
+        gain = [keep.tile([P, 2, HALF], F32, name="gain%d" % n) for n in range(2)]
+        gain_crossed = [keep.tile([P, 2, HALF], F32, name="gain_crossed%d" % n) for n in range(2)]
 
         def load_gain(n):
             nc.sync.dma_start(
@@ -139,7 +140,16 @@ def tile_gemma3mhattention_pa_kernel(
                 out=gain_psum[:, 0:DH], lhsT=ones[:], rhs=gain_rows[n][:], start=True, stop=True
             )
             nc.scalar.activation(
-                out=gain[n][:], in_=gain_psum[:, 0:DH], func=ACT.Identity, scale=scale, bias=scale
+                out=gain[n][:].rearrange("p a j -> p (a j)"), in_=gain_psum[:, 0:DH],
+                func=ACT.Identity, scale=scale, bias=scale,
+            )
+            nc.scalar.activation(
+                out=gain_crossed[n][:, 0, :], in_=gain_psum[:, HALF:DH], func=ACT.Identity,
+                scale=-scale, bias=-scale,
+            )
+            nc.scalar.activation(
+                out=gain_crossed[n][:, 1, :], in_=gain_psum[:, 0:HALF], func=ACT.Identity,
+                scale=scale, bias=scale,
             )
 
         eps = keep.tile([P, 1], F32)
@@ -290,7 +300,7 @@ def tile_gemma3mhattention_pa_kernel(
                 )
             return acc
 
-        def norm_and_rope(i, c, acc, cos_table, sin_table):
+        def norm_and_rope(i, c, acc, table, last):
             squares = stage.tile([P, CHUNK], BF16)
             sum_squares = stage.tile([P, CHUNK_HEADS], F32)
             for h in range(CHUNK_HEADS):
@@ -304,42 +314,42 @@ def tile_gemma3mhattention_pa_kernel(
                 out=rstd[:], in_=sum_squares[:], func=ACT.Abs_reciprocal_sqrt, bias=eps[:],
                 scale=1.0 / DH,
             )
-            straight = results.tile([P, CHUNK_HEADS, 2, HALF], F32)
-            crossed = stage.tile([P, CHUNK_HEADS, 2, HALF], F32)
-            for product, table in ((straight, cos_table), (crossed, sin_table)):
-                for h in range(CHUNK_HEADS):
-                    nc.vector.scalar_tensor_tensor(
-                        out=product[:, h].rearrange("p a j -> p (a j)"),
-                        in0=acc[:, h * DH : (h + 1) * DH],
-                        scalar=rstd[:, h : h + 1],
-                        in1=table[:, i, :],
-                        op0=ALU.mult,
-                        op1=ALU.mult,
-                    )
-            for a, op in ((0, ALU.subtract), (1, ALU.add)):
-                nc.gpsimd.tensor_tensor(
-                    out=straight[:, :, a, :], in0=straight[:, :, a, :], in1=crossed[:, :, 1 - a, :],
-                    op=op,
+            products = stage.tile([P, CHUNK_HEADS, 4, HALF], F32)
+            for h in range(CHUNK_HEADS):
+                nc.vector.scalar_tensor_tensor(
+                    out=products[:, h].rearrange("p (o a) j -> p o (a j)", o=2),
+                    in0=acc[:, h * DH : (h + 1) * DH].unsqueeze(1).to_broadcast([P, 2, DH]),
+                    scalar=rstd[:, h : h + 1],
+                    in1=table[:, i].rearrange("p (o a) j -> p o (a j)", o=2),
+                    op0=ALU.mult,
+                    op1=ALU.mult,
                 )
-            nc.sync.dma_start(out=chunk_out[c][i], in_=straight[:].rearrange("p h a j -> p h (a j)"))
+            rotated = results.tile([P, CHUNK_HEADS, 2, HALF], F32)
+            pairs_of_blocks = products[:].rearrange("p h (o a) j -> p h o a j", o=2)
+            adder = nc.vector if last else nc.gpsimd
+            adder.tensor_tensor(
+                out=rotated[:], in0=pairs_of_blocks[:, :, :, 0, :], in1=pairs_of_blocks[:, :, :, 1, :],
+                op=ALU.add,
+            )
+            nc.sync.dma_start(out=chunk_out[c][i], in_=rotated[:].rearrange("p h o j -> p h (o j)"))
 
         def copy_out(i, c, acc):
             plain = results.tile([P, CHUNK_HEADS, DH], F32)
             nc.scalar.copy(out=plain[:].rearrange("p h d -> p (h d)"), in_=acc[:])
             nc.sync.dma_start(out=chunk_out[c][i], in_=plain[:])
 
-        tables = [
-            [keep.tile([P, TILES, DH], F32, name="%s_table%d" % (name, n)) for name in ("sin", "cos")]
-            for n in range(2)
-        ]
+        tables = [keep.tile([P, TILES, 4, HALF], F32, name="table%d" % n) for n in range(2)]
 
         def fill_tables(n, engine, first, last):
             shape = [P, last - first, 2, HALF]
-            for trig, table in zip((sin, cos), tables[n]):
+            for trig, factor, blocks in (
+                (sin, gain_crossed[n], slice(1, 3)),
+                (cos, gain[n], slice(0, 4, 3)),
+            ):
                 engine.tensor_tensor(
-                    out=table[:, first:last, :].rearrange("p i (a j) -> p i a j", a=2),
+                    out=tables[n][:, first:last, blocks, :],
                     in0=trig[:, first:last, :].unsqueeze(2).to_broadcast(shape),
-                    in1=gain[n][:].rearrange("p (a j) -> p a j", a=2).unsqueeze(1).to_broadcast(shape),
+                    in1=factor[:].unsqueeze(1).to_broadcast(shape),
                     op=ALU.mult,
                 )
 
@@ -357,7 +367,7 @@ def tile_gemma3mhattention_pa_kernel(
                 if i == 0 and c == 2:
                     fill_tables(1, nc.vector, 0, K_TABLES_SPLIT)
                 if c < CHUNKS - 1:
-                    norm_and_rope(i, c, acc, chunk_tables[c][1], chunk_tables[c][0])
+                    norm_and_rope(i, c, acc, chunk_tables[c], i == TILES - 1 and c == CHUNKS - 2)
                 else:
                     copy_out(i, c, acc)
                 if c == 0 and i + 1 < TILES:

@@ -300,7 +300,7 @@ def tile_gemma3mhattention_pa_kernel(
                 )
             return acc
 
-        def norm_and_rope(i, c, acc, table, last):
+        def inverse_rms(acc):
             squares = stage.tile([P, CHUNK], BF16)
             sum_squares = stage.tile([P, CHUNK_HEADS], F32)
             for h in range(CHUNK_HEADS):
@@ -314,8 +314,14 @@ def tile_gemma3mhattention_pa_kernel(
                 out=rstd[:], in_=sum_squares[:], func=ACT.Abs_reciprocal_sqrt, bias=eps[:],
                 scale=1.0 / DH,
             )
+            return rstd
+
+        def rope(i, c, acc, rstd, table, last, next_halves):
+            next_operand = None
             products = stage.tile([P, CHUNK_HEADS, 4, HALF], F32)
             for h in range(CHUNK_HEADS):
+                if h == CHUNK_HEADS - 1 and next_halves is not None:
+                    next_operand = quantise(next_halves)
                 nc.vector.scalar_tensor_tensor(
                     out=products[:, h].rearrange("p (o a) j -> p o (a j)", o=2),
                     in0=acc[:, h * DH : (h + 1) * DH].unsqueeze(1).to_broadcast([P, 2, DH]),
@@ -332,6 +338,7 @@ def tile_gemma3mhattention_pa_kernel(
                 op=ALU.add,
             )
             nc.sync.dma_start(out=chunk_out[c][i], in_=rotated[:].rearrange("p h o j -> p h (o j)"))
+            return next_operand
 
         def copy_out(i, c, acc):
             plain = results.tile([P, CHUNK_HEADS, DH], F32)
@@ -366,9 +373,11 @@ def tile_gemma3mhattention_pa_kernel(
                     fill_tables(1, nc.gpsimd, K_TABLES_SPLIT, TILES)
                 if i == 0 and c == 2:
                     fill_tables(1, nc.vector, 0, K_TABLES_SPLIT)
-                if c < CHUNKS - 1:
-                    norm_and_rope(i, c, acc, chunk_tables[c], i == TILES - 1 and c == CHUNKS - 2)
-                else:
+                if c == CHUNKS - 1:
                     copy_out(i, c, acc)
-                if c == 0 and i + 1 < TILES:
-                    operand = quantise(transpose(i + 1))
+                elif c == 0 and i + 1 < TILES:
+                    rstd = inverse_rms(acc)
+                    operand = rope(i, c, acc, rstd, chunk_tables[c], False, transpose(i + 1))
+                else:
+                    last = i == TILES - 1 and c == CHUNKS - 2
+                    rope(i, c, acc, inverse_rms(acc), chunk_tables[c], last, None)

import math
from contextlib import ExitStack

import concourse.mybir as mybir
from concourse.masks import make_identity

F32 = mybir.dt.float32
BF16 = mybir.dt.bfloat16
I32 = mybir.dt.int32
U32 = mybir.dt.uint32
U8 = mybir.dt.uint8
FP8X4 = mybir.dt.float8_e4m3fn_x4
FP4X4 = mybir.dt.float4_e2m1fn_x4
ALU = mybir.AluOpType
ACT = mybir.ActivationFunctionType

P = 128
PACK = 4
K_PASS = P * PACK
T = 1024
E = 2048
DH = 128
HALF = DH // 2
SPREAD = 4
POSITION_EXCESS = 9.0
TILES = T // P
PASSES = E // K_PASS
CHUNK = 512
CHUNK_HEADS = CHUNK // DH
CHUNKS = 4
K_TABLES_SPLIT = 2
ROPE_THETA = 10000.0
EPS = 1e-6
Q_SCALE = DH**-0.5
TWO_PI = 2.0 * math.pi
ROUND_MAGIC = 1.5 * 2.0**23

FLOPS = 2 * T * E * (CHUNKS * CHUNK)

assert SPREAD**3 == HALF


def tile_gemma3mhattention_pa_kernel(
    tc,
    x,
    wq_words,
    wq_scales,
    wk_words,
    wk_scales,
    wv_words,
    wv_scales,
    q_norm_w,
    k_norm_w,
    out_0,
    out_1,
    out_2,
):
    nc = tc.nc

    x_by_tile = x[0].rearrange("(p i) k -> i p k", i=TILES)
    q_by_tile = out_0[0].rearrange("h (p i) d -> i p h d", i=TILES)
    k_by_tile = out_1[0].rearrange("h (p i) d -> i p h d", i=TILES)
    v_by_tile = out_2[0].rearrange("h (p i) d -> i p h d", i=TILES)
    chunk_words = [
        wq_words[:, :, 0 : 2 * CHUNK],
        wq_words[:, :, 2 * CHUNK : 4 * CHUNK],
        wk_words,
        wv_words,
    ]
    weight_scales = [wq_scales, wk_scales, wv_scales]
    chunk_out = [
        q_by_tile[:, :, 0:CHUNK_HEADS, :],
        q_by_tile[:, :, CHUNK_HEADS : 2 * CHUNK_HEADS, :],
        k_by_tile,
        v_by_tile,
    ]

    with ExitStack() as stack:
        stack.enter_context(tc.manual_schedule())
        keep = stack.enter_context(tc.tile_pool(name="keep", bufs=1))
        stage = stack.enter_context(tc.tile_pool(name="stage", bufs=3))
        results = stack.enter_context(tc.tile_pool(name="results", bufs=6))
        psum_xt = stack.enter_context(tc.psum_pool(name="psum_xt", bufs=2))
        psum_acc = stack.enter_context(tc.psum_pool(name="psum_acc", bufs=6))

        x_tiles = [keep.tile([P, E], BF16, name="x%d" % i) for i in range(TILES)]
        w_words = [
            keep.tile([P, PASSES, 2 * CHUNK], U8, name="w_words%d" % c, align_bytes=64)
            for c in range(CHUNKS)
        ]
        plane_tiles = [
            keep.tile([P, PASSES, width], U8, name="planes_%s" % name, align_bytes=64)
            for name, width in (("q", 2 * CHUNK), ("k", CHUNK), ("v", CHUNK))
        ]
        w_planes = [
            plane_tiles[0][:, :, 0:CHUNK],
            plane_tiles[0][:, :, CHUNK : 2 * CHUNK],
            plane_tiles[1][:],
            plane_tiles[2][:],
        ]

        def load_x(i, pieces):
            width = E // pieces
            for piece in range(pieces):
                columns = slice(piece * width, (piece + 1) * width)
                nc.sync.dma_start(out=x_tiles[i][:, columns], in_=x_by_tile[i][:, columns])

        def load_words(c):
            nc.sync.dma_start(
                out=w_words[c][:].bitcast(I32),
                in_=chunk_words[c].rearrange("g p b -> p g b").bitcast(I32),
            )

        def load_scales(n):
            if n == 0:
                nc.vector.memset(plane_tiles[n][:].bitcast(I32), 0)
            else:
                nc.gpsimd.memset(plane_tiles[n][:].bitcast(F32), 0.0)
            for quadrant in range(4):
                nc.sync.dma_start(
                    out=plane_tiles[n][32 * quadrant : 32 * quadrant + 4].bitcast(I32),
                    in_=weight_scales[n][:, 4 * quadrant : 4 * quadrant + 4, :]
                    .rearrange("g r n -> r g n")
                    .bitcast(I32),
                )

        gain_rows = [keep.tile([P, DH], BF16, name="gain_rows%d" % n) for n in range(2)]
        gain = [keep.tile([P, 2, HALF], F32, name="gain%d" % n) for n in range(2)]
        gain_crossed = [keep.tile([P, 2, HALF], F32, name="gain_crossed%d" % n) for n in range(2)]

        def load_gain(n):
            nc.sync.dma_start(
                out=gain_rows[n][0:1, :], in_=(q_norm_w, k_norm_w)[n].rearrange("(o d) -> o d", o=1)
            )

        def spread_gain(n):
            scale = (Q_SCALE, 1.0)[n]
            gain_psum = psum_acc.tile([P, CHUNK], F32, tag="acc")
            nc.tensor.matmul(
                out=gain_psum[:, 0:DH], lhsT=ones[:], rhs=gain_rows[n][:], start=True, stop=True
            )
            nc.scalar.activation(
                out=gain[n][:].rearrange("p a j -> p (a j)"), in_=gain_psum[:, 0:DH],
                func=ACT.Identity, scale=scale, bias=scale,
            )
            nc.scalar.activation(
                out=gain_crossed[n][:, 0, :], in_=gain_psum[:, HALF:DH], func=ACT.Identity,
                scale=-scale, bias=-scale,
            )
            nc.scalar.activation(
                out=gain_crossed[n][:, 1, :], in_=gain_psum[:, 0:HALF], func=ACT.Identity,
                scale=scale, bias=scale,
            )

        eps = keep.tile([P, 1], F32)
        nc.vector.memset(eps[:], EPS)
        warm = keep.tile([P, 1], F32)
        nc.scalar.activation(out=warm[:], in_=eps[:], func=ACT.Sin)
        nc.vector.memset(gain_rows[0][:], 0.0)

        load_x(0, 2)
        load_gain(0)
        load_scales(0)
        load_words(0)
        load_x(1, 1)

        up_to = keep.tile([P, P], BF16)
        nc.gpsimd.memset(up_to[:], 1.0)
        nc.gpsimd.affine_select(
            out=up_to[:], in_=up_to[:], compare_op=ALU.is_ge, fill=0.0, base=0, pattern=[[1, P]],
            channel_multiplier=-1,
        )
        identity = keep.tile([P, P], F32)
        make_identity(nc, identity[:])
        ones = keep.tile([P, P], BF16)
        nc.vector.memset(ones[:], 1.0)
        eights = keep.tile([P, TILES], BF16)
        nc.vector.memset(eights[:], float(TILES))
        nc.vector.memset(gain_rows[1][:], 0.0)
        position_psum = psum_acc.tile([P, CHUNK], F32, tag="acc")
        nc.tensor.matmul(
            out=position_psum[:, 0:TILES], lhsT=up_to[:], rhs=eights[:], start=True, stop=False
        )
        nc.tensor.matmul(
            out=position_psum[:, 0:TILES], lhsT=ones[:], rhs=up_to[:, 0:TILES], start=False, stop=True
        )

        load_gain(1)
        load_words(1)
        load_scales(1)
        load_scales(2)
        load_words(2)
        load_words(3)
        for i in range(2, TILES):
            load_x(i, 1)

        def transpose(i):
            pairs = x_tiles[i][:].bitcast(F32)
            halves = []
            for first in range(0, PASSES, 2):
                transposed = psum_xt.tile([P, 2, 2, P], F32)
                for g in range(2):
                    start = (first + g) * (K_PASS // 2)
                    for u in range(2):
                        nc.tensor.transpose(
                            transposed[:, g, u, :],
                            pairs[:, start + u : start + K_PASS // 2 : 2],
                            identity[:],
                        )
                grouped = stage.tile([P, 2, P, PACK], BF16, align_bytes=64)
                nc.scalar.copy(
                    out=grouped[:].bitcast(F32), in_=transposed[:].rearrange("p g u m -> p g m u")
                )
                halves.append((first, grouped))
            return halves

        def quantise(halves):
            x_words = stage.tile([P, PASSES, P], U32, align_bytes=64)
            x_planes = stage.tile([P, PASSES, P], U8, align_bytes=64)
            for first, grouped in halves:
                nc.vector.quantize_mx(
                    out=x_words[:, first : first + 2, :].rearrange("p g m -> p (g m)").bitcast(FP8X4),
                    scales=x_planes[:, first : first + 2, :].rearrange("p g m -> p (g m)"),
                    in_=grouped[:].rearrange("p g m t -> p (g m t)"),
                )
            return x_words, x_planes

        spread_gain(0)
        first_halves = transpose(0)

        turns_per_step = keep.tile([P, HALF], F32)
        one = keep.tile([P, 1], F32)
        nc.vector.memset(one[:], 1.0)
        for j in range(SPREAD):
            nc.vector.tensor_scalar(
                out=turns_per_step[:, j : j + 1],
                in0=one[:],
                scalar1=ROPE_THETA ** (-j / HALF) / TWO_PI,
                scalar2=None,
                op0=ALU.mult,
            )
        for width in (SPREAD, SPREAD * SPREAD):
            for copy in range(1, SPREAD):
                nc.vector.tensor_scalar(
                    out=turns_per_step[:, copy * width : (copy + 1) * width],
                    in0=turns_per_step[:, 0:width],
                    scalar1=ROPE_THETA ** (-copy * width / HALF),
                    scalar2=None,
                    op0=ALU.mult,
                )
        position = keep.tile([P, TILES], F32)
        nc.vector.tensor_scalar(
            out=position[:],
            in0=position_psum[:, 0:TILES],
            scalar1=-POSITION_EXCESS,
            scalar2=None,
            op0=ALU.add,
        )

        table_shape = [P, TILES, HALF]
        turns = keep.tile(table_shape, F32)
        nc.vector.tensor_tensor(
            out=turns[:],
            in0=position[:].unsqueeze(2).to_broadcast(table_shape),
            in1=turns_per_step[:].unsqueeze(1).to_broadcast(table_shape),
            op=ALU.mult,
        )
        whole_turns = keep.tile(table_shape, F32)
        nc.vector.tensor_scalar(
            out=whole_turns[:],
            in0=turns[:],
            scalar1=ROUND_MAGIC,
            scalar2=ROUND_MAGIC,
            op0=ALU.add,
            op1=ALU.subtract,
        )
        part = keep.tile(table_shape, F32)
        nc.vector.tensor_tensor(out=part[:], in0=turns[:], in1=whole_turns[:], op=ALU.subtract)
        abs_part = keep.tile(table_shape, F32)
        nc.scalar.activation(out=abs_part[:], in_=part[:], func=ACT.Abs)
        sin = keep.tile(table_shape, F32)
        nc.scalar.activation(out=sin[:], in_=part[:], func=ACT.Sin, scale=TWO_PI)
        cos = keep.tile(table_shape, F32)
        nc.scalar.activation(
            out=cos[:], in_=abs_part[:], func=ACT.Sin, scale=-TWO_PI, bias=math.pi / 2.0
        )
        nc.scalar.activation(out=warm[:], in_=eps[:], func=ACT.Abs_reciprocal_sqrt)

        def project(x_words, x_planes, c):
            acc = psum_acc.tile([P, CHUNK], F32)
            for g in range(PASSES):
                nc.tensor.matmul_mx(
                    out=acc[:],
                    lhsT=x_words[:, g, :].bitcast(FP8X4),
                    lhsT_scale=x_planes[:, g, :],
                    rhs=w_words[c][:, g, :].bitcast(FP4X4),
                    rhs_scale=w_planes[c][:, g, :],
                    start=(g == 0),
                    stop=(g == PASSES - 1),
                )
            return acc

        def inverse_rms(acc):
            squares = stage.tile([P, CHUNK], BF16)
            sum_squares = stage.tile([P, CHUNK_HEADS], F32)
            for h in range(CHUNK_HEADS):
                head = slice(h * DH, (h + 1) * DH)
                nc.scalar.activation(
                    out=squares[:, head], in_=acc[:, head], func=ACT.Square,
                    accum_out=sum_squares[:, h : h + 1],
                )
            rstd = stage.tile([P, CHUNK_HEADS], F32)
            nc.scalar.activation(
                out=rstd[:], in_=sum_squares[:], func=ACT.Abs_reciprocal_sqrt, bias=eps[:],
                scale=1.0 / DH,
            )
            return rstd

        def rope(i, c, acc, rstd, table, last, next_halves):
            next_operand = None
            products = stage.tile([P, CHUNK_HEADS, 4, HALF], F32)
            for h in range(CHUNK_HEADS):
                if h == CHUNK_HEADS - 1 and next_halves is not None:
                    next_operand = quantise(next_halves)
                nc.vector.scalar_tensor_tensor(
                    out=products[:, h].rearrange("p (o a) j -> p o (a j)", o=2),
                    in0=acc[:, h * DH : (h + 1) * DH].unsqueeze(1).to_broadcast([P, 2, DH]),
                    scalar=rstd[:, h : h + 1],
                    in1=table[:, i].rearrange("p (o a) j -> p o (a j)", o=2),
                    op0=ALU.mult,
                    op1=ALU.mult,
                )
            rotated = results.tile([P, CHUNK_HEADS, 2, HALF], F32)
            pairs_of_blocks = products[:].rearrange("p h (o a) j -> p h o a j", o=2)
            adder = nc.vector if last else nc.gpsimd
            adder.tensor_tensor(
                out=rotated[:], in0=pairs_of_blocks[:, :, :, 0, :], in1=pairs_of_blocks[:, :, :, 1, :],
                op=ALU.add,
            )
            nc.sync.dma_start(out=chunk_out[c][i], in_=rotated[:].rearrange("p h o j -> p h (o j)"))
            return next_operand

        def copy_out(i, c, acc):
            plain = results.tile([P, CHUNK_HEADS, DH], F32)
            nc.scalar.copy(out=plain[:].rearrange("p h d -> p (h d)"), in_=acc[:])
            nc.sync.dma_start(out=chunk_out[c][i], in_=plain[:])

        tables = [keep.tile([P, TILES, 4, HALF], F32, name="table%d" % n) for n in range(2)]

        def fill_tables(n, engine, first, last):
            shape = [P, last - first, 2, HALF]
            for trig, factor, blocks in (
                (sin, gain_crossed[n], slice(1, 3)),
                (cos, gain[n], slice(0, 4, 3)),
            ):
                engine.tensor_tensor(
                    out=tables[n][:, first:last, blocks, :],
                    in0=trig[:, first:last, :].unsqueeze(2).to_broadcast(shape),
                    in1=factor[:].unsqueeze(1).to_broadcast(shape),
                    op=ALU.mult,
                )

        operand = quantise(first_halves)
        fill_tables(0, nc.vector, 0, TILES)
        chunk_tables = [tables[0], tables[0], tables[1]]

        for i in range(TILES):
            x_words, x_planes = operand
            for c in range(CHUNKS):
                acc = project(x_words, x_planes, c)
                if i == 0 and c == 0:
                    spread_gain(1)
                    fill_tables(1, nc.gpsimd, K_TABLES_SPLIT, TILES)
                if i == 0 and c == 2:
                    fill_tables(1, nc.vector, 0, K_TABLES_SPLIT)
                if c == CHUNKS - 1:
                    copy_out(i, c, acc)
                elif c == 0 and i + 1 < TILES:
                    rstd = inverse_rms(acc)
                    operand = rope(i, c, acc, rstd, chunk_tables[c], False, transpose(i + 1))
                else:
                    last = i == TILES - 1 and c == CHUNKS - 2
                    rope(i, c, acc, inverse_rms(acc), chunk_tables[c], last, None)
